import numpy as np
import ml_dtypes

BF16 = ml_dtypes.bfloat16


def bf(x):
    return np.asarray(x, np.float32).astype(BF16)


def f32(x):
    return np.asarray(x, np.float32)


def f64(x):
    return np.asarray(x).astype(np.float64)


def striped(idx):
    return np.tile(idx.reshape(-1, 16).T, (8, 1))


C, S, N, T = 1024, 512, 256, 256
SCALE = 1.0 / np.sqrt(C)


def setup_inputs():
    return {"query": f32(np.random.standard_normal((C, N))), "keys": f32(np.random.standard_normal((C, T))), "values": bf(4.0 * np.random.standard_normal((T, C))), "mask": f32(np.random.random((T, N)) < 0.5), "rel": f32(0.25 * np.random.standard_normal((C, 1))), "base": f32(0.3 * np.random.standard_normal((C, S))), "offs": striped(np.random.permutation(S)[:N])}


def reference(query, keys, values, mask, rel, base, offs):
    idx = offs[:16].T.reshape(-1)
    qr = f64(query) + f64(rel)
    kr = f64(keys) + f64(rel)
    e = np.exp(SCALE * (kr.T @ qr))
    z = e.sum(axis=0, keepdims=True)
    u = f64(values).T @ (e * f64(mask))
    out = f64(base).copy()
    out[:, idx] = u * (1.0 / z)
    return out

@@ -1,0 +1,121 @@
+import concourse.mybir as mybir
+from concourse.masks import make_identity
+
+F32 = mybir.dt.float32
+BF16 = mybir.dt.bfloat16
+U16 = mybir.dt.uint16
+ADD = mybir.AluOpType.add
+MULT = mybir.AluOpType.mult
+FUNC = mybir.ActivationFunctionType
+
+P = 128
+C, S, N, T = 1024, 512, 256, 256
+SCALE = 0.03125
+D_BLOCKS = C // P
+C_BLOCKS = C // P
+J_BLOCKS = N // P
+T_BLOCKS = T // P
+LOAD_BLOCKS = 2
+
+FLOPS = 2 * C * T * N + 2 * T * C * N
+
+
+def tile_scaled_dot_product_attention_kernel(tc, query, keys, values, mask, rel, base, offs, out):
+    nc = tc.nc
+    with (
+        tc.tile_pool(name="held", bufs=1) as held,
+        tc.psum_pool(name="psum", bufs=1) as psum,
+        tc.psum_pool(name="psum_u", bufs=3) as psum_u,
+        tc.tile_pool(name="sbuf_u", bufs=3) as sbuf_u,
+    ):
+        offsets = held.tile([P, N // 16], U16, name="offsets")
+        nc.sync.dma_start(offsets[:], offs)
+
+        rel_sb = held.tile([P, D_BLOCKS], F32, name="rel_sb")
+        nc.sync.dma_start(rel_sb[:], rel.rearrange("(p b) one -> p (b one)", b=D_BLOCKS))
+        query_blocks = query.rearrange("(p b) j -> p b j", b=D_BLOCKS)
+        keys_blocks = keys.rearrange("(p b) t -> p b t", b=D_BLOCKS)
+        query_f32, keys_f32 = [], []
+        for first in range(0, D_BLOCKS, LOAD_BLOCKS):
+            q_load = held.tile([P, LOAD_BLOCKS, N], F32, name=f"query_f32_{first}")
+            k_load = held.tile([P, LOAD_BLOCKS, T], F32, name=f"keys_f32_{first}")
+            nc.sync.dma_start(q_load[:], query_blocks[:, first : first + LOAD_BLOCKS, :])
+            nc.scalar.dma_start(k_load[:], keys_blocks[:, first : first + LOAD_BLOCKS, :])
+            for k in range(LOAD_BLOCKS):
+                query_f32.append(q_load[:, k, :])
+                keys_f32.append(k_load[:, k, :])
+
+        mask_sb = held.tile([P, T_BLOCKS, N], F32, name="mask_sb")
+        nc.sync.dma_start(mask_sb[:], mask.rearrange("(tb p) j -> p tb j", p=P))
+        values_sb = held.tile([P, T_BLOCKS, C], BF16, name="values_sb")
+        nc.sync.dma_start(values_sb[:], values.rearrange("(tb p) c -> p tb c", p=P))
+
+        windows = []
+        for cb in range(C_BLOCKS):
+            window = held.tile([P, S], F32, name=f"window{cb}")
+            nc.sync.dma_start(window[:], base[cb * P : (cb + 1) * P, :])
+            windows.append(window)
+
+        identity_bf16 = held.tile([P, P], BF16, name="identity_bf16")
+        make_identity(nc, identity_bf16[:])
+        identity_f32 = held.tile([P, P], F32, name="identity_f32")
+        make_identity(nc, identity_f32[:])
+
+        att = [psum.tile([P, T], F32, name=f"att{jb}") for jb in range(J_BLOCKS)]
+        for b in range(D_BLOCKS):
+            keys_rel = held.tile([P, T], BF16, name=f"keys_rel{b}")
+            nc.vector.tensor_scalar(keys_rel[:], keys_f32[b], rel_sb[:, b : b + 1], SCALE, ADD, MULT)
+            query_rel = held.tile([P, N], BF16, name=f"query_rel{b}")
+            nc.scalar.activation(query_rel[:], query_f32[b], FUNC.Identity, bias=rel_sb[:, b : b + 1])
+            for jb in range(J_BLOCKS):
+                nc.tensor.matmul(
+                    att[jb][:],
+                    query_rel[:, jb * P : (jb + 1) * P],
+                    keys_rel[:],
+                    start=(b == 0),
+                    stop=(b == D_BLOCKS - 1),
+                )
+
+        neg_max = held.tile([P, J_BLOCKS], F32, name="neg_max")
+        z_sum = held.tile([P, J_BLOCKS], F32, name="z_sum")
+        e_tj = [psum.tile([P, N], BF16, name=f"e_tj{tb}") for tb in range(T_BLOCKS)]
+        for jb in range(J_BLOCKS):
+            nc.vector.reduce_max(neg_max[:, jb : jb + 1], att[jb][:], mybir.AxisListType.X, negate=True)
+            e_jt = held.tile([P, T], BF16, name=f"e_jt{jb}")
+            nc.scalar.activation(
+                e_jt[:], att[jb][:], FUNC.Exp, bias=neg_max[:, jb : jb + 1], accum_out=z_sum[:, jb : jb + 1]
+            )
+            for tb in range(T_BLOCKS):
+                nc.tensor.transpose(e_tj[tb][:, jb * P : (jb + 1) * P], e_jt[:, tb * P : (tb + 1) * P], identity_bf16[:])
+
+        z_inv = held.tile([P, J_BLOCKS], F32, name="z_inv")
+        nc.vector.reciprocal(z_inv[:], z_sum[:])
+        z_inv_columns = held.tile([P, J_BLOCKS, P], F32, name="z_inv_columns")
+        nc.vector.tensor_copy(z_inv_columns[:], z_inv[:].unsqueeze(2).to_broadcast([P, J_BLOCKS, P]))
+
+        e_masked = []
+        for tb in range(T_BLOCKS):
+            em_block = held.tile([P, N], BF16, name=f"e_masked{tb}")
+            nc.vector.tensor_tensor(em_block[:], e_tj[tb][:], mask_sb[:, tb, :], MULT)
+            e_masked.append(em_block)
+
+        z_inv_psum = psum.tile([P, N], F32, name="z_inv_psum")
+        for jb in range(J_BLOCKS):
+            nc.tensor.transpose(z_inv_psum[:, jb * P : (jb + 1) * P], z_inv_columns[:, jb, :], identity_f32[:])
+        z_inv_rows = held.tile([P, N], F32, name="z_inv_rows")
+        nc.scalar.copy(z_inv_rows[:], z_inv_psum[:])
+
+        for cb in range(C_BLOCKS):
+            u_psum = psum_u.tile([P, N], F32, name="u_psum")
+            for tb in range(T_BLOCKS):
+                nc.tensor.matmul(
+                    u_psum[:],
+                    values_sb[:, tb, cb * P : (cb + 1) * P],
+                    e_masked[tb][:],
+                    start=(tb == 0),
+                    stop=(tb == T_BLOCKS - 1),
+                )
+            u_sb = sbuf_u.tile([P, N], F32, name="u_sb")
+            nc.scalar.copy(u_sb[:], u_psum[:])
+            nc.vector.tensor_tensor(windows[cb][:].indirect(offsets[:]), u_sb[:], z_inv_rows[:], MULT)
+            nc.sync.dma_start(out[cb * P : (cb + 1) * P, :], windows[cb][:])

@@ -28,6 +28,10 @@ def tile_scaled_dot_product_attention_kernel(tc, query, keys, values, mask, rel,
         tc.psum_pool(name="psum_u", bufs=3) as psum_u,
         tc.tile_pool(name="sbuf_u", bufs=3) as sbuf_u,
     ):
+        scratch = held.tile([P, 1], F32, name="scratch")
+        nc.vector.memset(scratch[:], 0.0)
+        nc.scalar.activation(scratch[:], scratch[:], FUNC.Exp)
+
         offsets = held.tile([P, N // 16], U16, name="offsets")
         nc.sync.dma_start(offsets[:], offs)
 

@@ -13,113 +13,133 @@ C, S, N, T = 1024, 512, 256, 256
 SCALE = 0.03125
 D_BLOCKS = C // P
 C_BLOCKS = C // P
-J_BLOCKS = N // P
 T_BLOCKS = T // P
-LOAD_BLOCKS = 2
+KEY_LOAD = 2
+QUERY_LOAD = 4
 
 FLOPS = 2 * C * T * N + 2 * T * C * N
+
+
+def load_query_half(pool, query, half, queues):
+    query_blocks = query.rearrange("(p b) j -> p b j", b=D_BLOCKS)
+    blocks = []
+    for first, queue in zip(range(0, D_BLOCKS, QUERY_LOAD), queues):
+        q_load = pool.tile([P, QUERY_LOAD, P], F32, name=f"query_f32_{half}_{first}")
+        queue.dma_start(q_load[:], query_blocks[:, first : first + QUERY_LOAD, half * P : (half + 1) * P])
+        for k in range(QUERY_LOAD):
+            blocks.append(q_load[:, k, :])
+    return blocks
 
 
 def tile_scaled_dot_product_attention_kernel(tc, query, keys, values, mask, rel, base, offs, out):
     nc = tc.nc
     with (
         tc.tile_pool(name="held", bufs=1) as held,
-        tc.psum_pool(name="psum", bufs=1) as psum,
-        tc.psum_pool(name="psum_u", bufs=3) as psum_u,
         tc.tile_pool(name="sbuf_u", bufs=3) as sbuf_u,
+        tc.psum_pool(name="psum", bufs=1) as psum,
+        tc.psum_pool(name="psum_u", bufs=2) as psum_u,
     ):
         scratch = held.tile([P, 1], F32, name="scratch")
         nc.vector.memset(scratch[:], 0.0)
         nc.scalar.activation(scratch[:], scratch[:], FUNC.Exp)
 
-        offsets = held.tile([P, N // 16], U16, name="offsets")
-        nc.sync.dma_start(offsets[:], offs)
-
         rel_sb = held.tile([P, D_BLOCKS], F32, name="rel_sb")
         nc.sync.dma_start(rel_sb[:], rel.rearrange("(p b) one -> p (b one)", b=D_BLOCKS))
-        query_blocks = query.rearrange("(p b) j -> p b j", b=D_BLOCKS)
+        query_f32 = [load_query_half(held, query, 0, (nc.sync, nc.scalar))]
+
         keys_blocks = keys.rearrange("(p b) t -> p b t", b=D_BLOCKS)
-        query_f32, keys_f32 = [], []
-        for first in range(0, D_BLOCKS, LOAD_BLOCKS):
-            q_load = held.tile([P, LOAD_BLOCKS, N], F32, name=f"query_f32_{first}")
-            k_load = held.tile([P, LOAD_BLOCKS, T], F32, name=f"keys_f32_{first}")
-            nc.sync.dma_start(q_load[:], query_blocks[:, first : first + LOAD_BLOCKS, :])
-            nc.scalar.dma_start(k_load[:], keys_blocks[:, first : first + LOAD_BLOCKS, :])
-            for k in range(LOAD_BLOCKS):
-                query_f32.append(q_load[:, k, :])
+        keys_f32 = []
+        for first in range(0, D_BLOCKS, KEY_LOAD):
+            k_load = held.tile([P, KEY_LOAD, T], F32, name=f"keys_f32_{first}")
+            queue = nc.sync if (first // KEY_LOAD) % 2 == 0 else nc.scalar
+            queue.dma_start(k_load[:], keys_blocks[:, first : first + KEY_LOAD, :])
+            for k in range(KEY_LOAD):
                 keys_f32.append(k_load[:, k, :])
 
         mask_sb = held.tile([P, T_BLOCKS, N], F32, name="mask_sb")
         nc.sync.dma_start(mask_sb[:], mask.rearrange("(tb p) j -> p tb j", p=P))
         values_sb = held.tile([P, T_BLOCKS, C], BF16, name="values_sb")
-        nc.sync.dma_start(values_sb[:], values.rearrange("(tb p) c -> p tb c", p=P))
+        nc.scalar.dma_start(values_sb[:], values.rearrange("(tb p) c -> p tb c", p=P))
+        offsets = held.tile([P, N // 16], U16, name="offsets")
+        nc.sync.dma_start(offsets[:], offs)
 
-        windows = []
-        for cb in range(C_BLOCKS):
-            window = held.tile([P, S], F32, name=f"window{cb}")
-            nc.sync.dma_start(window[:], base[cb * P : (cb + 1) * P, :])
-            windows.append(window)
+        windows = [held.tile([P, S], F32, name=f"window{cb}") for cb in range(C_BLOCKS)]
+        for cb in range(2):
+            nc.scalar.dma_start(windows[cb][:], base[cb * P : (cb + 1) * P, :])
+        query_f32.append(load_query_half(held, query, 1, (nc.sync, nc.sync)))
+        for cb in range(2, C_BLOCKS):
+            nc.sync.dma_start(windows[cb][:], base[cb * P : (cb + 1) * P, :])
 
         identity_bf16 = held.tile([P, P], BF16, name="identity_bf16")
         make_identity(nc, identity_bf16[:])
         identity_f32 = held.tile([P, P], F32, name="identity_f32")
         make_identity(nc, identity_f32[:])
 
-        att = [psum.tile([P, T], F32, name=f"att{jb}") for jb in range(J_BLOCKS)]
+        keys_rel = []
         for b in range(D_BLOCKS):
-            keys_rel = held.tile([P, T], BF16, name=f"keys_rel{b}")
-            nc.vector.tensor_scalar(keys_rel[:], keys_f32[b], rel_sb[:, b : b + 1], SCALE, ADD, MULT)
-            query_rel = held.tile([P, N], BF16, name=f"query_rel{b}")
-            nc.scalar.activation(query_rel[:], query_f32[b], FUNC.Identity, bias=rel_sb[:, b : b + 1])
-            for jb in range(J_BLOCKS):
-                nc.tensor.matmul(
-                    att[jb][:],
-                    query_rel[:, jb * P : (jb + 1) * P],
-                    keys_rel[:],
-                    start=(b == 0),
-                    stop=(b == D_BLOCKS - 1),
-                )
+            kr_block = held.tile([P, T], BF16, name=f"keys_rel{b}")
+            nc.vector.tensor_scalar(kr_block[:], keys_f32[b], rel_sb[:, b : b + 1], None, ADD)
+            keys_rel.append(kr_block)
 
-        neg_max = held.tile([P, J_BLOCKS], F32, name="neg_max")
-        z_sum = held.tile([P, J_BLOCKS], F32, name="z_sum")
-        e_tj = [psum.tile([P, N], BF16, name=f"e_tj{tb}") for tb in range(T_BLOCKS)]
-        for jb in range(J_BLOCKS):
-            nc.vector.reduce_max(neg_max[:, jb : jb + 1], att[jb][:], mybir.AxisListType.X, negate=True)
-            e_jt = held.tile([P, T], BF16, name=f"e_jt{jb}")
-            nc.scalar.activation(
-                e_jt[:], att[jb][:], FUNC.Exp, bias=neg_max[:, jb : jb + 1], accum_out=z_sum[:, jb : jb + 1]
-            )
+        def exponentials(half, adder):
+            att = psum.tile([P, T], F32, name=f"att{half}")
+            for b in range(D_BLOCKS):
+                query_rel = held.tile([P, P], BF16, name=f"query_rel{half}_{b}")
+                adder.tensor_scalar(query_rel[:], query_f32[half][b], rel_sb[:, b : b + 1], SCALE, ADD, MULT)
+                nc.tensor.matmul(att[:], query_rel[:], keys_rel[b][:], start=(b == 0), stop=(b == D_BLOCKS - 1))
+            neg_max = held.tile([P, 1], F32, name=f"neg_max{half}")
+            nc.vector.reduce_max(neg_max[:], att[:], mybir.AxisListType.X, negate=True)
+            e_jt = held.tile([P, T], BF16, name=f"e_jt{half}")
+            z_sum = held.tile([P, 1], F32, name=f"z_sum{half}")
+            nc.scalar.activation(e_jt[:], att[:], FUNC.Exp, bias=neg_max[:], accum_out=z_sum[:])
+            e_tj = psum.tile([P, T_BLOCKS, P], BF16, name=f"e_tj{half}")
             for tb in range(T_BLOCKS):
-                nc.tensor.transpose(e_tj[tb][:, jb * P : (jb + 1) * P], e_jt[:, tb * P : (tb + 1) * P], identity_bf16[:])
+                nc.tensor.transpose(e_tj[:, tb, :], e_jt[:, tb * P : (tb + 1) * P], identity_bf16[:])
+            return e_tj, z_sum
 
-        z_inv = held.tile([P, J_BLOCKS], F32, name="z_inv")
-        nc.vector.reciprocal(z_inv[:], z_sum[:])
-        z_inv_columns = held.tile([P, J_BLOCKS, P], F32, name="z_inv_columns")
-        nc.vector.tensor_copy(z_inv_columns[:], z_inv[:].unsqueeze(2).to_broadcast([P, J_BLOCKS, P]))
+        def rows_of_z_inv(half, z_sum):
+            z_inv = held.tile([P, 1], F32, name=f"z_inv{half}")
+            nc.vector.reciprocal(z_inv[:], z_sum[:])
+            z_inv_columns = held.tile([P, P], F32, name=f"z_inv_columns{half}")
+            nc.vector.tensor_copy(z_inv_columns[:], z_inv[:].to_broadcast([P, P]))
+            z_inv_psum = psum.tile([P, P], F32, name=f"z_inv_psum{half}")
+            nc.tensor.transpose(z_inv_psum[:], z_inv_columns[:], identity_f32[:])
+            z_inv_rows = held.tile([P, P], F32, name=f"z_inv_rows{half}")
+            nc.scalar.copy(z_inv_rows[:], z_inv_psum[:])
+            return z_inv_rows
 
-        e_masked = []
-        for tb in range(T_BLOCKS):
-            em_block = held.tile([P, N], BF16, name=f"e_masked{tb}")
-            nc.vector.tensor_tensor(em_block[:], e_tj[tb][:], mask_sb[:, tb, :], MULT)
-            e_masked.append(em_block)
+        def masked(half, e_tj):
+            e_masked = held.tile([P, T_BLOCKS, P], BF16, name=f"e_masked{half}")
+            nc.vector.tensor_tensor(e_masked[:], e_tj[:], mask_sb[:, :, half * P : (half + 1) * P], MULT)
+            return e_masked
 
-        z_inv_psum = psum.tile([P, N], F32, name="z_inv_psum")
-        for jb in range(J_BLOCKS):
-            nc.tensor.transpose(z_inv_psum[:, jb * P : (jb + 1) * P], z_inv_columns[:, jb, :], identity_f32[:])
-        z_inv_rows = held.tile([P, N], F32, name="z_inv_rows")
-        nc.scalar.copy(z_inv_rows[:], z_inv_psum[:])
-
-        for cb in range(C_BLOCKS):
-            u_psum = psum_u.tile([P, N], F32, name="u_psum")
+        def place(half, cb, e_masked, z_inv_rows):
+            u_psum = psum_u.tile([P, P], F32, name="u_psum")
             for tb in range(T_BLOCKS):
                 nc.tensor.matmul(
                     u_psum[:],
                     values_sb[:, tb, cb * P : (cb + 1) * P],
-                    e_masked[tb][:],
+                    e_masked[:, tb, :],
                     start=(tb == 0),
                     stop=(tb == T_BLOCKS - 1),
                 )
-            u_sb = sbuf_u.tile([P, N], F32, name="u_sb")
+            u_sb = sbuf_u.tile([P, P], F32, name="u_sb")
             nc.scalar.copy(u_sb[:], u_psum[:])
-            nc.vector.tensor_tensor(windows[cb][:].indirect(offsets[:]), u_sb[:], z_inv_rows[:], MULT)
+            piece = offsets[:, half * (P // 16) : (half + 1) * (P // 16)]
+            nc.vector.tensor_tensor(windows[cb][:].indirect(piece), u_sb[:], z_inv_rows[:], MULT)
+
+        e_tj_0, z_sum_0 = exponentials(0, nc.vector)
+        z_inv_rows_0 = rows_of_z_inv(0, z_sum_0)
+        e_masked_0 = masked(0, e_tj_0)
+        for cb in range(C_BLOCKS // 2):
+            place(0, cb, e_masked_0, z_inv_rows_0)
+        e_tj_1, z_sum_1 = exponentials(1, nc.gpsimd)
+        place(0, C_BLOCKS // 2, e_masked_0, z_inv_rows_0)
+        z_inv_rows_1 = rows_of_z_inv(1, z_sum_1)
+        place(0, C_BLOCKS // 2 + 1, e_masked_0, z_inv_rows_0)
+        e_masked_1 = masked(1, e_tj_1)
+        for cb in range(C_BLOCKS // 2 + 2, C_BLOCKS):
+            place(0, cb, e_masked_0, z_inv_rows_0)
+        for cb in range(C_BLOCKS):
+            place(1, cb, e_masked_1, z_inv_rows_1)
             nc.sync.dma_start(out[cb * P : (cb + 1) * P, :], windows[cb][:])

@@ -13,108 +13,104 @@ C, S, N, T = 1024, 512, 256, 256
 SCALE = 0.03125
 D_BLOCKS = C // P
 C_BLOCKS = C // P
+J_BLOCKS = N // P
 T_BLOCKS = T // P
-KEY_LOAD = 2
-QUERY_LOAD = 4
+LOAD_BLOCKS = 2
 
 FLOPS = 2 * C * T * N + 2 * T * C * N
-
-
-def load_query_half(pool, query, half, queues):
-    query_blocks = query.rearrange("(p b) j -> p b j", b=D_BLOCKS)
-    blocks = []
-    for first, queue in zip(range(0, D_BLOCKS, QUERY_LOAD), queues):
-        q_load = pool.tile([P, QUERY_LOAD, P], F32, name=f"query_f32_{half}_{first}")
-        queue.dma_start(q_load[:], query_blocks[:, first : first + QUERY_LOAD, half * P : (half + 1) * P])
-        for k in range(QUERY_LOAD):
-            blocks.append(q_load[:, k, :])
-    return blocks
 
 
 def tile_scaled_dot_product_attention_kernel(tc, query, keys, values, mask, rel, base, offs, out):
     nc = tc.nc
     with (
         tc.tile_pool(name="held", bufs=1) as held,
-        tc.tile_pool(name="sbuf_u", bufs=3) as sbuf_u,
         tc.psum_pool(name="psum", bufs=1) as psum,
-        tc.psum_pool(name="psum_u", bufs=2) as psum_u,
+        tc.psum_pool(name="psum_u", bufs=3) as psum_u,
+        tc.tile_pool(name="sbuf_u", bufs=3) as sbuf_u,
     ):
         scratch = held.tile([P, 1], F32, name="scratch")
         nc.vector.memset(scratch[:], 0.0)
         nc.scalar.activation(scratch[:], scratch[:], FUNC.Exp)
 
-        rel_sb = held.tile([P, D_BLOCKS], F32, name="rel_sb")
-        nc.sync.dma_start(rel_sb[:], rel.rearrange("(p b) one -> p (b one)", b=D_BLOCKS))
-        query_f32 = [load_query_half(held, query, 0, (nc.sync, nc.scalar))]
-
-        keys_blocks = keys.rearrange("(p b) t -> p b t", b=D_BLOCKS)
-        keys_f32 = []
-        for first in range(0, D_BLOCKS, KEY_LOAD):
-            k_load = held.tile([P, KEY_LOAD, T], F32, name=f"keys_f32_{first}")
-            queue = nc.sync if (first // KEY_LOAD) % 2 == 0 else nc.scalar
-            queue.dma_start(k_load[:], keys_blocks[:, first : first + KEY_LOAD, :])
-            for k in range(KEY_LOAD):
-                keys_f32.append(k_load[:, k, :])
-
-        mask_sb = held.tile([P, T_BLOCKS, N], F32, name="mask_sb")
-        nc.sync.dma_start(mask_sb[:], mask.rearrange("(tb p) j -> p tb j", p=P))
-        values_sb = held.tile([P, T_BLOCKS, C], BF16, name="values_sb")
-        nc.scalar.dma_start(values_sb[:], values.rearrange("(tb p) c -> p tb c", p=P))
         offsets = held.tile([P, N // 16], U16, name="offsets")
         nc.sync.dma_start(offsets[:], offs)
 
-        windows = [held.tile([P, S], F32, name=f"window{cb}") for cb in range(C_BLOCKS)]
-        for cb in range(2):
-            nc.scalar.dma_start(windows[cb][:], base[cb * P : (cb + 1) * P, :])
-        query_f32.append(load_query_half(held, query, 1, (nc.sync, nc.sync)))
-        for cb in range(2, C_BLOCKS):
-            nc.sync.dma_start(windows[cb][:], base[cb * P : (cb + 1) * P, :])
+        rel_sb = held.tile([P, D_BLOCKS], F32, name="rel_sb")
+        nc.sync.dma_start(rel_sb[:], rel.rearrange("(p b) one -> p (b one)", b=D_BLOCKS))
+        query_blocks = query.rearrange("(p b) j -> p b j", b=D_BLOCKS)
+        keys_blocks = keys.rearrange("(p b) t -> p b t", b=D_BLOCKS)
+        query_f32, keys_f32 = [], []
+        for first in range(0, D_BLOCKS, LOAD_BLOCKS):
+            q_load = held.tile([P, LOAD_BLOCKS, N], F32, name=f"query_f32_{first}")
+            k_load = held.tile([P, LOAD_BLOCKS, T], F32, name=f"keys_f32_{first}")
+            nc.sync.dma_start(q_load[:], query_blocks[:, first : first + LOAD_BLOCKS, :])
+            nc.scalar.dma_start(k_load[:], keys_blocks[:, first : first + LOAD_BLOCKS, :])
+            for k in range(LOAD_BLOCKS):
+                query_f32.append(q_load[:, k, :])
+                keys_f32.append(k_load[:, k, :])
+
+        mask_f32 = held.tile([P, T_BLOCKS, N], F32, name="mask_f32")
+        nc.sync.dma_start(mask_f32[:], mask.rearrange("(tb p) j -> p tb j", p=P))
+        values_sb = held.tile([P, T_BLOCKS, C], BF16, name="values_sb")
+        nc.sync.dma_start(values_sb[:], values.rearrange("(tb p) c -> p tb c", p=P))
+
+        windows = []
+        for cb in range(C_BLOCKS):
+            window = held.tile([P, S], F32, name=f"window{cb}")
+            nc.sync.dma_start(window[:], base[cb * P : (cb + 1) * P, :])
+            windows.append(window)
 
         identity_bf16 = held.tile([P, P], BF16, name="identity_bf16")
         make_identity(nc, identity_bf16[:])
         identity_f32 = held.tile([P, P], F32, name="identity_f32")
         make_identity(nc, identity_f32[:])
 
-        keys_rel = []
-        for b in range(D_BLOCKS):
-            kr_block = held.tile([P, T], BF16, name=f"keys_rel{b}")
-            nc.vector.tensor_scalar(kr_block[:], keys_f32[b], rel_sb[:, b : b + 1], None, ADD)
-            keys_rel.append(kr_block)
+        mask_bf16 = held.tile([P, T_BLOCKS, N], BF16, name="mask_bf16")
+        nc.gpsimd.tensor_copy(mask_bf16[:], mask_f32[:])
 
-        def exponentials(half, adder):
-            att = psum.tile([P, T], F32, name=f"att{half}")
-            for b in range(D_BLOCKS):
-                query_rel = held.tile([P, P], BF16, name=f"query_rel{half}_{b}")
-                adder.tensor_scalar(query_rel[:], query_f32[half][b], rel_sb[:, b : b + 1], SCALE, ADD, MULT)
-                nc.tensor.matmul(att[:], query_rel[:], keys_rel[b][:], start=(b == 0), stop=(b == D_BLOCKS - 1))
-            neg_max = held.tile([P, 1], F32, name=f"neg_max{half}")
-            nc.vector.reduce_max(neg_max[:], att[:], mybir.AxisListType.X, negate=True)
-            e_jt = held.tile([P, T], BF16, name=f"e_jt{half}")
-            z_sum = held.tile([P, 1], F32, name=f"z_sum{half}")
-            nc.scalar.activation(e_jt[:], att[:], FUNC.Exp, bias=neg_max[:], accum_out=z_sum[:])
-            e_tj = psum.tile([P, T_BLOCKS, P], BF16, name=f"e_tj{half}")
+        att = [psum.tile([P, T], F32, name=f"att{jb}") for jb in range(J_BLOCKS)]
+        for b in range(D_BLOCKS):
+            keys_rel = held.tile([P, T], BF16, name=f"keys_rel{b}")
+            nc.vector.tensor_scalar(keys_rel[:], keys_f32[b], rel_sb[:, b : b + 1], SCALE, ADD, MULT)
+            query_rel = held.tile([P, N], BF16, name=f"query_rel{b}")
+            nc.scalar.activation(query_rel[:], query_f32[b], FUNC.Identity, bias=rel_sb[:, b : b + 1])
+            for jb in range(J_BLOCKS):
+                nc.tensor.matmul(
+                    att[jb][:],
+                    query_rel[:, jb * P : (jb + 1) * P],
+                    keys_rel[:],
+                    start=(b == 0),
+                    stop=(b == D_BLOCKS - 1),
+                )
+
+        neg_max = held.tile([P, J_BLOCKS], F32, name="neg_max")
+        for jb in range(J_BLOCKS):
+            nc.vector.reduce_max(neg_max[:, jb : jb + 1], att[jb][:], mybir.AxisListType.X, negate=True)
+        e_masked = held.tile([P, T_BLOCKS, N], BF16, name="e_masked")
+        z_inv_psum = psum.tile([P, N], F32, name="z_inv_psum")
+        for jb in range(J_BLOCKS):
+            queries = slice(jb * P, (jb + 1) * P)
+            e_jt = held.tile([P, T], BF16, name=f"e_jt{jb}")
+            z_sum = held.tile([P, 1], F32, name=f"z_sum{jb}")
+            nc.scalar.activation(e_jt[:], att[jb][:], FUNC.Exp, bias=neg_max[:, jb : jb + 1], accum_out=z_sum[:])
+
+            e_tj = psum.tile([P, T_BLOCKS, P], BF16, name=f"e_tj{jb}")
             for tb in range(T_BLOCKS):
                 nc.tensor.transpose(e_tj[:, tb, :], e_jt[:, tb * P : (tb + 1) * P], identity_bf16[:])
-            return e_tj, z_sum
 
-        def rows_of_z_inv(half, z_sum):
-            z_inv = held.tile([P, 1], F32, name=f"z_inv{half}")
+            z_inv = held.tile([P, 1], F32, name=f"z_inv{jb}")
             nc.vector.reciprocal(z_inv[:], z_sum[:])
-            z_inv_columns = held.tile([P, P], F32, name=f"z_inv_columns{half}")
+            z_inv_columns = held.tile([P, P], F32, name=f"z_inv_columns{jb}")
             nc.vector.tensor_copy(z_inv_columns[:], z_inv[:].to_broadcast([P, P]))
-            z_inv_psum = psum.tile([P, P], F32, name=f"z_inv_psum{half}")
-            nc.tensor.transpose(z_inv_psum[:], z_inv_columns[:], identity_f32[:])
-            z_inv_rows = held.tile([P, P], F32, name=f"z_inv_rows{half}")
-            nc.scalar.copy(z_inv_rows[:], z_inv_psum[:])
-            return z_inv_rows
+            nc.tensor.transpose(z_inv_psum[:, queries], z_inv_columns[:], identity_f32[:])
 
-        def masked(half, e_tj):
-            e_masked = held.tile([P, T_BLOCKS, P], BF16, name=f"e_masked{half}")
-            nc.vector.tensor_tensor(e_masked[:], e_tj[:], mask_sb[:, :, half * P : (half + 1) * P], MULT)
-            return e_masked
+            nc.vector.tensor_tensor(e_masked[:, :, queries], e_tj[:], mask_bf16[:, :, queries], MULT)
 
-        def place(half, cb, e_masked, z_inv_rows):
-            u_psum = psum_u.tile([P, P], F32, name="u_psum")
+        z_inv_rows = held.tile([P, N], F32, name="z_inv_rows")
+        nc.vector.tensor_copy(z_inv_rows[:], z_inv_psum[:])
+
+        for cb in range(C_BLOCKS):
+            u_psum = psum_u.tile([P, N], F32, name="u_psum")
             for tb in range(T_BLOCKS):
                 nc.tensor.matmul(
                     u_psum[:],
@@ -123,23 +119,7 @@ def tile_scaled_dot_product_attention_kernel(tc, query, keys, values, mask, rel,
                     start=(tb == 0),
                     stop=(tb == T_BLOCKS - 1),
                 )
-            u_sb = sbuf_u.tile([P, P], F32, name="u_sb")
+            u_sb = sbuf_u.tile([P, N], F32, name="u_sb")
             nc.scalar.copy(u_sb[:], u_psum[:])
-            piece = offsets[:, half * (P // 16) : (half + 1) * (P // 16)]
-            nc.vector.tensor_tensor(windows[cb][:].indirect(piece), u_sb[:], z_inv_rows[:], MULT)
-
-        e_tj_0, z_sum_0 = exponentials(0, nc.vector)
-        z_inv_rows_0 = rows_of_z_inv(0, z_sum_0)
-        e_masked_0 = masked(0, e_tj_0)
-        for cb in range(C_BLOCKS // 2):
-            place(0, cb, e_masked_0, z_inv_rows_0)
-        e_tj_1, z_sum_1 = exponentials(1, nc.gpsimd)
-        place(0, C_BLOCKS // 2, e_masked_0, z_inv_rows_0)
-        z_inv_rows_1 = rows_of_z_inv(1, z_sum_1)
-        place(0, C_BLOCKS // 2 + 1, e_masked_0, z_inv_rows_0)
-        e_masked_1 = masked(1, e_tj_1)
-        for cb in range(C_BLOCKS // 2 + 2, C_BLOCKS):
-            place(0, cb, e_masked_0, z_inv_rows_0)
-        for cb in range(C_BLOCKS):
-            place(1, cb, e_masked_1, z_inv_rows_1)
+            nc.vector.tensor_tensor(windows[cb][:].indirect(offsets[:]), u_sb[:], z_inv_rows[:], MULT)
             nc.sync.dma_start(out[cb * P : (cb + 1) * P, :], windows[cb][:])

@@ -28,13 +28,6 @@ def tile_scaled_dot_product_attention_kernel(tc, query, keys, values, mask, rel,
         tc.psum_pool(name="psum_u", bufs=3) as psum_u,
         tc.tile_pool(name="sbuf_u", bufs=3) as sbuf_u,
     ):
-        scratch = held.tile([P, 1], F32, name="scratch")
-        nc.vector.memset(scratch[:], 0.0)
-        nc.scalar.activation(scratch[:], scratch[:], FUNC.Exp)
-
-        offsets = held.tile([P, N // 16], U16, name="offsets")
-        nc.sync.dma_start(offsets[:], offs)
-
         rel_sb = held.tile([P, D_BLOCKS], F32, name="rel_sb")
         nc.sync.dma_start(rel_sb[:], rel.rearrange("(p b) one -> p (b one)", b=D_BLOCKS))
         query_blocks = query.rearrange("(p b) j -> p b j", b=D_BLOCKS)
@@ -53,12 +46,18 @@ def tile_scaled_dot_product_attention_kernel(tc, query, keys, values, mask, rel,
         nc.sync.dma_start(mask_f32[:], mask.rearrange("(tb p) j -> p tb j", p=P))
         values_sb = held.tile([P, T_BLOCKS, C], BF16, name="values_sb")
         nc.sync.dma_start(values_sb[:], values.rearrange("(tb p) c -> p tb c", p=P))
+        offsets = held.tile([P, N // 16], U16, name="offsets")
+        nc.sync.dma_start(offsets[:], offs)
 
         windows = []
         for cb in range(C_BLOCKS):
             window = held.tile([P, S], F32, name=f"window{cb}")
             nc.sync.dma_start(window[:], base[cb * P : (cb + 1) * P, :])
             windows.append(window)
+
+        scratch = held.tile([P, 1], F32, name="scratch")
+        nc.vector.memset(scratch[:], 0.0)
+        nc.scalar.activation(scratch[:], scratch[:], FUNC.Exp)
 
         identity_bf16 = held.tile([P, P], BF16, name="identity_bf16")
         make_identity(nc, identity_bf16[:])
@@ -73,7 +72,7 @@ def tile_scaled_dot_product_attention_kernel(tc, query, keys, values, mask, rel,
             keys_rel = held.tile([P, T], BF16, name=f"keys_rel{b}")
             nc.vector.tensor_scalar(keys_rel[:], keys_f32[b], rel_sb[:, b : b + 1], SCALE, ADD, MULT)
             query_rel = held.tile([P, N], BF16, name=f"query_rel{b}")
-            nc.scalar.activation(query_rel[:], query_f32[b], FUNC.Identity, bias=rel_sb[:, b : b + 1])
+            nc.vector.tensor_scalar(query_rel[:], query_f32[b], rel_sb[:, b : b + 1], None, ADD)
             for jb in range(J_BLOCKS):
                 nc.tensor.matmul(
                     att[jb][:],

@@ -42,8 +42,8 @@ def tile_scaled_dot_product_attention_kernel(tc, query, keys, values, mask, rel,
                 query_f32.append(q_load[:, k, :])
                 keys_f32.append(k_load[:, k, :])
 
-        mask_f32 = held.tile([P, T_BLOCKS, N], F32, name="mask_f32")
-        nc.sync.dma_start(mask_f32[:], mask.rearrange("(tb p) j -> p tb j", p=P))
+        mask_sb = held.tile([P, T_BLOCKS, N], F32, name="mask_sb")
+        nc.sync.dma_start(mask_sb[:], mask.rearrange("(tb p) j -> p tb j", p=P))
         values_sb = held.tile([P, T_BLOCKS, C], BF16, name="values_sb")
         nc.sync.dma_start(values_sb[:], values.rearrange("(tb p) c -> p tb c", p=P))
         offsets = held.tile([P, N // 16], U16, name="offsets")
@@ -64,9 +64,6 @@ def tile_scaled_dot_product_attention_kernel(tc, query, keys, values, mask, rel,
         identity_f32 = held.tile([P, P], F32, name="identity_f32")
         make_identity(nc, identity_f32[:])
 
-        mask_bf16 = held.tile([P, T_BLOCKS, N], BF16, name="mask_bf16")
-        nc.gpsimd.tensor_copy(mask_bf16[:], mask_f32[:])
-
         att = [psum.tile([P, T], F32, name=f"att{jb}") for jb in range(J_BLOCKS)]
         for b in range(D_BLOCKS):
             keys_rel = held.tile([P, T], BF16, name=f"keys_rel{b}")
@@ -83,30 +80,33 @@ def tile_scaled_dot_product_attention_kernel(tc, query, keys, values, mask, rel,
                 )
 
         neg_max = held.tile([P, J_BLOCKS], F32, name="neg_max")
+        z_sum = held.tile([P, J_BLOCKS], F32, name="z_sum")
+        e_tj = [psum.tile([P, N], BF16, name=f"e_tj{tb}") for tb in range(T_BLOCKS)]
         for jb in range(J_BLOCKS):
             nc.vector.reduce_max(neg_max[:, jb : jb + 1], att[jb][:], mybir.AxisListType.X, negate=True)
-        e_masked = held.tile([P, T_BLOCKS, N], BF16, name="e_masked")
+            e_jt = held.tile([P, T], BF16, name=f"e_jt{jb}")
+            nc.scalar.activation(
+                e_jt[:], att[jb][:], FUNC.Exp, bias=neg_max[:, jb : jb + 1], accum_out=z_sum[:, jb : jb + 1]
+            )
+            for tb in range(T_BLOCKS):
+                nc.tensor.transpose(e_tj[tb][:, jb * P : (jb + 1) * P], e_jt[:, tb * P : (tb + 1) * P], identity_bf16[:])
+
+        z_inv = held.tile([P, J_BLOCKS], F32, name="z_inv")
+        nc.vector.reciprocal(z_inv[:], z_sum[:])
+        z_inv_columns = held.tile([P, J_BLOCKS, P], F32, name="z_inv_columns")
+        nc.vector.tensor_copy(z_inv_columns[:], z_inv[:].unsqueeze(2).to_broadcast([P, J_BLOCKS, P]))
+
+        e_masked = []
+        for tb in range(T_BLOCKS):
+            em_block = held.tile([P, N], BF16, name=f"e_masked{tb}")
+            nc.vector.tensor_tensor(em_block[:], e_tj[tb][:], mask_sb[:, tb, :], MULT)
+            e_masked.append(em_block)
+
         z_inv_psum = psum.tile([P, N], F32, name="z_inv_psum")
         for jb in range(J_BLOCKS):
-            queries = slice(jb * P, (jb + 1) * P)
-            e_jt = held.tile([P, T], BF16, name=f"e_jt{jb}")
-            z_sum = held.tile([P, 1], F32, name=f"z_sum{jb}")
-            nc.scalar.activation(e_jt[:], att[jb][:], FUNC.Exp, bias=neg_max[:, jb : jb + 1], accum_out=z_sum[:])
-
-            e_tj = psum.tile([P, T_BLOCKS, P], BF16, name=f"e_tj{jb}")
-            for tb in range(T_BLOCKS):
-                nc.tensor.transpose(e_tj[:, tb, :], e_jt[:, tb * P : (tb + 1) * P], identity_bf16[:])
-
-            z_inv = held.tile([P, 1], F32, name=f"z_inv{jb}")
-            nc.vector.reciprocal(z_inv[:], z_sum[:])
-            z_inv_columns = held.tile([P, P], F32, name=f"z_inv_columns{jb}")
-            nc.vector.tensor_copy(z_inv_columns[:], z_inv[:].to_broadcast([P, P]))
-            nc.tensor.transpose(z_inv_psum[:, queries], z_inv_columns[:], identity_f32[:])
-
-            nc.vector.tensor_tensor(e_masked[:, :, queries], e_tj[:], mask_bf16[:, :, queries], MULT)
-
+            nc.tensor.transpose(z_inv_psum[:, jb * P : (jb + 1) * P], z_inv_columns[:, jb, :], identity_f32[:])
         z_inv_rows = held.tile([P, N], F32, name="z_inv_rows")
-        nc.vector.tensor_copy(z_inv_rows[:], z_inv_psum[:])
+        nc.scalar.copy(z_inv_rows[:], z_inv_psum[:])
 
         for cb in range(C_BLOCKS):
             u_psum = psum_u.tile([P, N], F32, name="u_psum")
@@ -114,7 +114,7 @@ def tile_scaled_dot_product_attention_kernel(tc, query, keys, values, mask, rel,
                 nc.tensor.matmul(
                     u_psum[:],
                     values_sb[:, tb, cb * P : (cb + 1) * P],
-                    e_masked[:, tb, :],
+                    e_masked[tb][:],
                     start=(tb == 0),
                     stop=(tb == T_BLOCKS - 1),
                 )

@@ -15,7 +15,8 @@ D_BLOCKS = C // P
 C_BLOCKS = C // P
 J_BLOCKS = N // P
 T_BLOCKS = T // P
-LOAD_BLOCKS = 2
+LOAD_BLOCKS = (2, 2, 2, 1, 1)
+assert sum(LOAD_BLOCKS) == D_BLOCKS
 
 FLOPS = 2 * C * T * N + 2 * T * C * N
 
@@ -33,14 +34,16 @@ def tile_scaled_dot_product_attention_kernel(tc, query, keys, values, mask, rel,
         query_blocks = query.rearrange("(p b) j -> p b j", b=D_BLOCKS)
         keys_blocks = keys.rearrange("(p b) t -> p b t", b=D_BLOCKS)
         query_f32, keys_f32 = [], []
-        for first in range(0, D_BLOCKS, LOAD_BLOCKS):
-            q_load = held.tile([P, LOAD_BLOCKS, N], F32, name=f"query_f32_{first}")
-            k_load = held.tile([P, LOAD_BLOCKS, T], F32, name=f"keys_f32_{first}")
-            nc.sync.dma_start(q_load[:], query_blocks[:, first : first + LOAD_BLOCKS, :])
-            nc.scalar.dma_start(k_load[:], keys_blocks[:, first : first + LOAD_BLOCKS, :])
-            for k in range(LOAD_BLOCKS):
+        first = 0
+        for blocks in LOAD_BLOCKS:
+            q_load = held.tile([P, blocks, N], F32, name=f"query_f32_{first}")
+            k_load = held.tile([P, blocks, T], F32, name=f"keys_f32_{first}")
+            nc.sync.dma_start(q_load[:], query_blocks[:, first : first + blocks, :])
+            nc.scalar.dma_start(k_load[:], keys_blocks[:, first : first + blocks, :])
+            for k in range(blocks):
                 query_f32.append(q_load[:, k, :])
                 keys_f32.append(k_load[:, k, :])
+            first += blocks
 
         mask_sb = held.tile([P, T_BLOCKS, N], F32, name="mask_sb")
         nc.sync.dma_start(mask_sb[:], mask.rearrange("(tb p) j -> p tb j", p=P))
@@ -79,15 +82,11 @@ def tile_scaled_dot_product_attention_kernel(tc, query, keys, values, mask, rel,
                     stop=(b == D_BLOCKS - 1),
                 )
 
-        neg_max = held.tile([P, J_BLOCKS], F32, name="neg_max")
         z_sum = held.tile([P, J_BLOCKS], F32, name="z_sum")
         e_tj = [psum.tile([P, N], BF16, name=f"e_tj{tb}") for tb in range(T_BLOCKS)]
         for jb in range(J_BLOCKS):
-            nc.vector.reduce_max(neg_max[:, jb : jb + 1], att[jb][:], mybir.AxisListType.X, negate=True)
             e_jt = held.tile([P, T], BF16, name=f"e_jt{jb}")
-            nc.scalar.activation(
-                e_jt[:], att[jb][:], FUNC.Exp, bias=neg_max[:, jb : jb + 1], accum_out=z_sum[:, jb : jb + 1]
-            )
+            nc.scalar.activation(e_jt[:], att[jb][:], FUNC.Exp, accum_out=z_sum[:, jb : jb + 1])
             for tb in range(T_BLOCKS):
                 nc.tensor.transpose(e_tj[tb][:, jb * P : (jb + 1) * P], e_jt[:, tb * P : (tb + 1) * P], identity_bf16[:])
 

@@ -47,6 +47,8 @@ def tile_scaled_dot_product_attention_kernel(tc, query, keys, values, mask, rel,
 
         mask_sb = held.tile([P, T_BLOCKS, N], F32, name="mask_sb")
         nc.sync.dma_start(mask_sb[:], mask.rearrange("(tb p) j -> p tb j", p=P))
+        mask_bf16 = held.tile([P, T_BLOCKS, N], BF16, name="mask_bf16")
+        nc.gpsimd.tensor_copy(mask_bf16[:], mask_sb[:])
         values_sb = held.tile([P, T_BLOCKS, C], BF16, name="values_sb")
         nc.sync.dma_start(values_sb[:], values.rearrange("(tb p) c -> p tb c", p=P))
         offsets = held.tile([P, N // 16], U16, name="offsets")
@@ -83,40 +85,36 @@ def tile_scaled_dot_product_attention_kernel(tc, query, keys, values, mask, rel,
                 )
 
         z_sum = held.tile([P, J_BLOCKS], F32, name="z_sum")
-        e_tj = [psum.tile([P, N], BF16, name=f"e_tj{tb}") for tb in range(T_BLOCKS)]
+        e_masked = []
         for jb in range(J_BLOCKS):
             e_jt = held.tile([P, T], BF16, name=f"e_jt{jb}")
             nc.scalar.activation(e_jt[:], att[jb][:], FUNC.Exp, accum_out=z_sum[:, jb : jb + 1])
+            e_tj = psum.tile([P, T_BLOCKS, P], BF16, name=f"e_tj{jb}")
             for tb in range(T_BLOCKS):
-                nc.tensor.transpose(e_tj[tb][:, jb * P : (jb + 1) * P], e_jt[:, tb * P : (tb + 1) * P], identity_bf16[:])
+                nc.tensor.transpose(e_tj[:, tb, :], e_jt[:, tb * P : (tb + 1) * P], identity_bf16[:])
+            em_block = held.tile([P, T_BLOCKS, P], BF16, name=f"e_masked{jb}")
+            nc.vector.tensor_tensor(em_block[:], e_tj[:], mask_bf16[:, :, jb * P : (jb + 1) * P], MULT)
+            e_masked.append(em_block)
 
         z_inv = held.tile([P, J_BLOCKS], F32, name="z_inv")
         nc.vector.reciprocal(z_inv[:], z_sum[:])
-        z_inv_columns = held.tile([P, J_BLOCKS, P], F32, name="z_inv_columns")
-        nc.vector.tensor_copy(z_inv_columns[:], z_inv[:].unsqueeze(2).to_broadcast([P, J_BLOCKS, P]))
-
-        e_masked = []
-        for tb in range(T_BLOCKS):
-            em_block = held.tile([P, N], BF16, name=f"e_masked{tb}")
-            nc.vector.tensor_tensor(em_block[:], e_tj[tb][:], mask_sb[:, tb, :], MULT)
-            e_masked.append(em_block)
-
         z_inv_psum = psum.tile([P, N], F32, name="z_inv_psum")
         for jb in range(J_BLOCKS):
-            nc.tensor.transpose(z_inv_psum[:, jb * P : (jb + 1) * P], z_inv_columns[:, jb, :], identity_f32[:])
+            nc.tensor.transpose(z_inv_psum[:, jb * P : (jb + 1) * P], z_inv[:, jb : jb + 1].to_broadcast([P, P]), identity_f32[:])
         z_inv_rows = held.tile([P, N], F32, name="z_inv_rows")
         nc.scalar.copy(z_inv_rows[:], z_inv_psum[:])
 
         for cb in range(C_BLOCKS):
             u_psum = psum_u.tile([P, N], F32, name="u_psum")
-            for tb in range(T_BLOCKS):
-                nc.tensor.matmul(
-                    u_psum[:],
-                    values_sb[:, tb, cb * P : (cb + 1) * P],
-                    e_masked[tb][:],
-                    start=(tb == 0),
-                    stop=(tb == T_BLOCKS - 1),
-                )
+            for jb in range(J_BLOCKS):
+                for tb in range(T_BLOCKS):
+                    nc.tensor.matmul(
+                        u_psum[:, jb * P : (jb + 1) * P],
+                        values_sb[:, tb, cb * P : (cb + 1) * P],
+                        e_masked[jb][:, tb, :],
+                        start=(tb == 0),
+                        stop=(tb == T_BLOCKS - 1),
+                    )
             u_sb = sbuf_u.tile([P, N], F32, name="u_sb")
             nc.scalar.copy(u_sb[:], u_psum[:])
             nc.vector.tensor_tensor(windows[cb][:].indirect(offsets[:]), u_sb[:], z_inv_rows[:], MULT)

@@ -48,7 +48,7 @@ def tile_scaled_dot_product_attention_kernel(tc, query, keys, values, mask, rel,
         mask_sb = held.tile([P, T_BLOCKS, N], F32, name="mask_sb")
         nc.sync.dma_start(mask_sb[:], mask.rearrange("(tb p) j -> p tb j", p=P))
         mask_bf16 = held.tile([P, T_BLOCKS, N], BF16, name="mask_bf16")
-        nc.gpsimd.tensor_copy(mask_bf16[:], mask_sb[:])
+        nc.vector.tensor_copy(mask_bf16[:], mask_sb[:])
         values_sb = held.tile([P, T_BLOCKS, C], BF16, name="values_sb")
         nc.sync.dma_start(values_sb[:], values.rearrange("(tb p) c -> p tb c", p=P))
         offsets = held.tile([P, N // 16], U16, name="offsets")

@@ -15,7 +15,7 @@ D_BLOCKS = C // P
 C_BLOCKS = C // P
 J_BLOCKS = N // P
 T_BLOCKS = T // P
-LOAD_BLOCKS = (2, 2, 2, 1, 1)
+LOAD_BLOCKS = (1, 2, 2, 1, 1, 1)
 assert sum(LOAD_BLOCKS) == D_BLOCKS
 
 FLOPS = 2 * C * T * N + 2 * T * C * N
@@ -30,7 +30,6 @@ def tile_scaled_dot_product_attention_kernel(tc, query, keys, values, mask, rel,
         tc.tile_pool(name="sbuf_u", bufs=3) as sbuf_u,
     ):
         rel_sb = held.tile([P, D_BLOCKS], F32, name="rel_sb")
-        nc.sync.dma_start(rel_sb[:], rel.rearrange("(p b) one -> p (b one)", b=D_BLOCKS))
         query_blocks = query.rearrange("(p b) j -> p b j", b=D_BLOCKS)
         keys_blocks = keys.rearrange("(p b) t -> p b t", b=D_BLOCKS)
         query_f32, keys_f32 = [], []
@@ -43,6 +42,8 @@ def tile_scaled_dot_product_attention_kernel(tc, query, keys, values, mask, rel,
             for k in range(blocks):
                 query_f32.append(q_load[:, k, :])
                 keys_f32.append(k_load[:, k, :])
+            if first == 0:
+                nc.sync.dma_start(rel_sb[:], rel.rearrange("(p b) one -> p (b one)", b=D_BLOCKS))
             first += blocks
 
         mask_sb = held.tile([P, T_BLOCKS, N], F32, name="mask_sb")
@@ -72,7 +73,7 @@ def tile_scaled_dot_product_attention_kernel(tc, query, keys, values, mask, rel,
         att = [psum.tile([P, T], F32, name=f"att{jb}") for jb in range(J_BLOCKS)]
         for b in range(D_BLOCKS):
             keys_rel = held.tile([P, T], BF16, name=f"keys_rel{b}")
-            nc.vector.tensor_scalar(keys_rel[:], keys_f32[b], rel_sb[:, b : b + 1], SCALE, ADD, MULT)
+            nc.vector.tensor_scalar(keys_rel[:], keys_f32[b], rel_sb[:, b : b + 1], None, ADD)
             query_rel = held.tile([P, N], BF16, name=f"query_rel{b}")
             nc.vector.tensor_scalar(query_rel[:], query_f32[b], rel_sb[:, b : b + 1], None, ADD)
             for jb in range(J_BLOCKS):
@@ -88,7 +89,7 @@ def tile_scaled_dot_product_attention_kernel(tc, query, keys, values, mask, rel,
         e_masked = []
         for jb in range(J_BLOCKS):
             e_jt = held.tile([P, T], BF16, name=f"e_jt{jb}")
-            nc.scalar.activation(e_jt[:], att[jb][:], FUNC.Exp, accum_out=z_sum[:, jb : jb + 1])
+            nc.scalar.activation(e_jt[:], att[jb][:], FUNC.Exp, scale=SCALE, accum_out=z_sum[:, jb : jb + 1])
             e_tj = psum.tile([P, T_BLOCKS, P], BF16, name=f"e_tj{jb}")
             for tb in range(T_BLOCKS):
                 nc.tensor.transpose(e_tj[:, tb, :], e_jt[:, tb * P : (tb + 1) * P], identity_bf16[:])

import concourse.mybir as mybir
from concourse.masks import make_identity

F32 = mybir.dt.float32
BF16 = mybir.dt.bfloat16
U16 = mybir.dt.uint16
ADD = mybir.AluOpType.add
MULT = mybir.AluOpType.mult
FUNC = mybir.ActivationFunctionType

P = 128
C, S, N, T = 1024, 512, 256, 256
SCALE = 0.03125
D_BLOCKS = C // P
C_BLOCKS = C // P
J_BLOCKS = N // P
T_BLOCKS = T // P
LOAD_BLOCKS = (1, 2, 2, 1, 1, 1)
assert sum(LOAD_BLOCKS) == D_BLOCKS

FLOPS = 2 * C * T * N + 2 * T * C * N


def tile_scaled_dot_product_attention_kernel(tc, query, keys, values, mask, rel, base, offs, out):
    nc = tc.nc
    with (
        tc.tile_pool(name="held", bufs=1) as held,
        tc.psum_pool(name="psum", bufs=1) as psum,
        tc.psum_pool(name="psum_u", bufs=3) as psum_u,
        tc.tile_pool(name="sbuf_u", bufs=3) as sbuf_u,
    ):
        rel_sb = held.tile([P, D_BLOCKS], F32, name="rel_sb")
        query_blocks = query.rearrange("(p b) j -> p b j", b=D_BLOCKS)
        keys_blocks = keys.rearrange("(p b) t -> p b t", b=D_BLOCKS)
        query_f32, keys_f32 = [], []
        first = 0
        for blocks in LOAD_BLOCKS:
            q_load = held.tile([P, blocks, N], F32, name=f"query_f32_{first}")
            k_load = held.tile([P, blocks, T], F32, name=f"keys_f32_{first}")
            nc.sync.dma_start(q_load[:], query_blocks[:, first : first + blocks, :])
            nc.scalar.dma_start(k_load[:], keys_blocks[:, first : first + blocks, :])
            for k in range(blocks):
                query_f32.append(q_load[:, k, :])
                keys_f32.append(k_load[:, k, :])
            if first == 0:
                nc.sync.dma_start(rel_sb[:], rel.rearrange("(p b) one -> p (b one)", b=D_BLOCKS))
            first += blocks

        mask_sb = held.tile([P, T_BLOCKS, N], F32, name="mask_sb")
        nc.sync.dma_start(mask_sb[:], mask.rearrange("(tb p) j -> p tb j", p=P))
        mask_bf16 = held.tile([P, T_BLOCKS, N], BF16, name="mask_bf16")
        nc.vector.tensor_copy(mask_bf16[:], mask_sb[:])
        values_sb = held.tile([P, T_BLOCKS, C], BF16, name="values_sb")
        nc.sync.dma_start(values_sb[:], values.rearrange("(tb p) c -> p tb c", p=P))
        offsets = held.tile([P, N // 16], U16, name="offsets")
        nc.sync.dma_start(offsets[:], offs)

        windows = []
        for cb in range(C_BLOCKS):
            window = held.tile([P, S], F32, name=f"window{cb}")
            nc.sync.dma_start(window[:], base[cb * P : (cb + 1) * P, :])
            windows.append(window)

        scratch = held.tile([P, 1], F32, name="scratch")
        nc.vector.memset(scratch[:], 0.0)
        nc.scalar.activation(scratch[:], scratch[:], FUNC.Exp)

        identity_bf16 = held.tile([P, P], BF16, name="identity_bf16")
        make_identity(nc, identity_bf16[:])
        identity_f32 = held.tile([P, P], F32, name="identity_f32")
        make_identity(nc, identity_f32[:])

        att = [psum.tile([P, T], F32, name=f"att{jb}") for jb in range(J_BLOCKS)]
        for b in range(D_BLOCKS):
            keys_rel = held.tile([P, T], BF16, name=f"keys_rel{b}")
            nc.vector.tensor_scalar(keys_rel[:], keys_f32[b], rel_sb[:, b : b + 1], None, ADD)
            query_rel = held.tile([P, N], BF16, name=f"query_rel{b}")
            nc.vector.tensor_scalar(query_rel[:], query_f32[b], rel_sb[:, b : b + 1], None, ADD)
            for jb in range(J_BLOCKS):
                nc.tensor.matmul(
                    att[jb][:],
                    query_rel[:, jb * P : (jb + 1) * P],
                    keys_rel[:],
                    start=(b == 0),
                    stop=(b == D_BLOCKS - 1),
                )

        z_sum = held.tile([P, J_BLOCKS], F32, name="z_sum")
        e_masked = []
        for jb in range(J_BLOCKS):
            e_jt = held.tile([P, T], BF16, name=f"e_jt{jb}")
            nc.scalar.activation(e_jt[:], att[jb][:], FUNC.Exp, scale=SCALE, accum_out=z_sum[:, jb : jb + 1])
            e_tj = psum.tile([P, T_BLOCKS, P], BF16, name=f"e_tj{jb}")
            for tb in range(T_BLOCKS):
                nc.tensor.transpose(e_tj[:, tb, :], e_jt[:, tb * P : (tb + 1) * P], identity_bf16[:])
            em_block = held.tile([P, T_BLOCKS, P], BF16, name=f"e_masked{jb}")
            nc.vector.tensor_tensor(em_block[:], e_tj[:], mask_bf16[:, :, jb * P : (jb + 1) * P], MULT)
            e_masked.append(em_block)

        z_inv = held.tile([P, J_BLOCKS], F32, name="z_inv")
        nc.vector.reciprocal(z_inv[:], z_sum[:])
        z_inv_psum = psum.tile([P, N], F32, name="z_inv_psum")
        for jb in range(J_BLOCKS):
            nc.tensor.transpose(z_inv_psum[:, jb * P : (jb + 1) * P], z_inv[:, jb : jb + 1].to_broadcast([P, P]), identity_f32[:])
        z_inv_rows = held.tile([P, N], F32, name="z_inv_rows")
        nc.scalar.copy(z_inv_rows[:], z_inv_psum[:])

        for cb in range(C_BLOCKS):
            u_psum = psum_u.tile([P, N], F32, name="u_psum")
            for jb in range(J_BLOCKS):
                for tb in range(T_BLOCKS):
                    nc.tensor.matmul(
                        u_psum[:, jb * P : (jb + 1) * P],
                        values_sb[:, tb, cb * P : (cb + 1) * P],
                        e_masked[jb][:, tb, :],
                        start=(tb == 0),
                        stop=(tb == T_BLOCKS - 1),
                    )
            u_sb = sbuf_u.tile([P, N], F32, name="u_sb")
            nc.scalar.copy(u_sb[:], u_psum[:])
            nc.vector.tensor_tensor(windows[cb][:].indirect(offsets[:]), u_sb[:], z_inv_rows[:], MULT)
            nc.sync.dma_start(out[cb * P : (cb + 1) * P, :], windows[cb][:])
